import numpy as np
import ml_dtypes


def mxq(x, axis, fmt="e4m3"):
    dtype, down = {"e4m3": (ml_dtypes.float8_e4m3fn, 7), "e5m2": (ml_dtypes.float8_e5m2, 14)}[fmt]
    v = np.moveaxis(np.asarray(x, np.float32).astype(ml_dtypes.bfloat16).astype(np.float64), axis, -1)
    blocks = v.reshape(v.shape[:-1] + (-1, 32))
    amax = np.abs(blocks).max(-1, keepdims=True)
    byte = np.maximum(np.where(amax > 0, np.frexp(amax)[1] - 1 + 127, 0) - down, 1)
    scale = np.exp2(byte - 127.0)
    codes = (blocks / scale).astype(np.float32).astype(dtype).astype(np.float64)
    return np.moveaxis((codes * scale).reshape(v.shape), -1, axis)


WIDE = False


def mx_kscale(k):
    if not WIDE:
        return np.ones(k)
    levels = np.array([10, -10, 5, -5, 0])
    a = np.random.permutation(np.resize(levels, k // 512 * 4)).reshape(k // 512, 4)
    idx = np.arange(k)
    return np.exp2(a[idx // 512, idx % 128 // 32])


BF16 = ml_dtypes.bfloat16


def bf(x):
    return np.asarray(x, np.float32).astype(BF16)


def f64(x):
    return np.asarray(x).astype(np.float64)


E2M1 = np.array([0.0, 0.5, 1.0, 1.5, 2.0, 3.0, 4.0, 6.0, -0.0, -0.5, -1.0, -1.5, -2.0, -3.0, -4.0, -6.0])


def pack_weight(w, fmt):
    k, n = w.shape
    w = f64(bf(w)).reshape(k // 32, 32, n)
    amax = np.abs(w).max(1)
    if fmt == "e4m3":
        byte = np.frexp(amax)[1] - 1 + 127 - 7
    else:
        mant, ex = np.frexp(amax / 6.0)
        byte = np.where(mant > 0.5, ex, ex - 1) + 127
    byte = np.clip(np.where(amax > 0, byte, 1), 1, 254)
    scaled = (w * np.exp2(127.0 - byte)[:, None, :]).reshape(k, n).astype(np.float32)
    by_word = np.ascontiguousarray(scaled.reshape(k // 512, 128, 4, n).transpose(0, 1, 3, 2))
    if fmt == "e4m3":
        words = by_word.astype(ml_dtypes.float8_e4m3fn).view(np.uint8)
    else:
        c = by_word.astype(ml_dtypes.float4_e2m1fn).view(np.uint8) & 0xF
        words = c[..., 0::2] | (c[..., 1::2] << 4)
    return np.ascontiguousarray(words), np.ascontiguousarray(byte.astype(np.uint8).reshape(k // 512, 16, n))


def unpack_weight(words, scales, fmt):
    g, p, n, _ = words.shape
    if fmt == "e4m3":
        vals = np.ascontiguousarray(words).view(ml_dtypes.float8_e4m3fn).astype(np.float64)
    else:
        nib = np.empty((g, p, n, 4), np.uint8)
        nib[..., 0::2] = words & 0xF
        nib[..., 1::2] = words >> 4
        vals = E2M1[nib]
    vals = vals * np.repeat(np.exp2(scales.astype(np.float64) - 127.0), 8, axis=1)[..., None]
    return vals.transpose(0, 1, 3, 2).reshape(g * 512, n)

def pack4(w):
    words, scales = pack_weight(w, "e2m1")
    return words.reshape(words.shape[0], 128, -1), scales


def unpack4(words, scales):
    return unpack_weight(words.reshape(words.shape[0], 128, -1, 2), scales, "e2m1")


B, N, D1, D2, F1, F2, F3, F4 = 8192, 1, 256, 256, 512, 64, 32, 16
K = D1 + D2
EPS = 1e-5
SLOPE = 0.2


def setup_inputs():
    s = mx_kscale(K)
    g = np.sqrt(EPS)
    input1 = bf(np.random.standard_normal((B, N, D1)) * s[:D1])
    input2 = bf(np.random.standard_normal((B, N, D2)) * s[D1:])
    w1 = np.random.standard_normal((F1, K)) * 5.0 * g / np.sqrt(K) / s[None, :]
    words, scales = pack4(np.ascontiguousarray(w1.T))
    b1 = bf(np.random.standard_normal(F1) * 2.5 * g)
    return {"input1": input1,
            "input2": input2,
            "W1_words": words,
            "W1_scales": scales,
            "b1": b1}


def reference(input1, input2, W1_words, W1_scales, b1):
    x = np.concatenate([f64(input1), f64(input2)], axis=2)
    h = (mxq(x, 2, "e4m3") @ unpack4(W1_words, W1_scales)) + f64(b1)
    m = h.mean(axis=-1, keepdims=True)
    v = np.square(h - m).mean(axis=-1, keepdims=True)
    hn = (h - m) * (1.0 / np.sqrt(v + EPS))
    return np.where(hn >= 0, hn, SLOPE * hn)

@@ -1,0 +1,279 @@
+from contextlib import ExitStack
+
+import concourse.mybir as mybir
+from concourse.masks import make_identity
+
+F32 = mybir.dt.float32
+BF16 = mybir.dt.bfloat16
+I32 = mybir.dt.int32
+U32 = mybir.dt.uint32
+U8 = mybir.dt.uint8
+FP8X4 = mybir.dt.float8_e4m3fn_x4
+FP4X4 = mybir.dt.float4_e2m1fn_x4
+ACT = mybir.ActivationFunctionType
+ALU = mybir.AluOpType
+
+P = 128
+ROWS = 8192
+D_IN = 256
+K = 2 * D_IN
+WORDS = K // 2
+FEATURES = 512
+EPS = 1e-5
+SLOPE = 0.2
+
+TILES = 4
+PAIRS = TILES // 2
+N_GROUPS = ROWS // (TILES * P)
+
+FLOPS = 2 * ROWS * K * FEATURES
+
+
+def tile_fcd_pa_t_kernel(tc, input1, input2, W1_words, W1_scales, b1, out):
+    nc = tc.nc
+
+    x1_groups = input1.rearrange("(g p j) o d -> g p j (o d)", p=P, j=TILES)
+    x2_groups = input2.rearrange("(g p j) o d -> g p j (o d)", p=P, j=TILES)
+    out_groups = out.rearrange("(g p j) o f -> g p j (o f)", p=P, j=TILES)
+
+    with ExitStack() as ctx:
+        const = ctx.enter_context(tc.tile_pool(name="const", bufs=1))
+        x_pool = ctx.enter_context(tc.tile_pool(name="x", bufs=1))
+        quant = ctx.enter_context(tc.tile_pool(name="quant", bufs=2))
+        h_pool = ctx.enter_context(tc.tile_pool(name="h", bufs=3))
+        y_pool = ctx.enter_context(tc.tile_pool(name="y", bufs=3))
+        out_pool = ctx.enter_context(tc.tile_pool(name="out", bufs=4))
+        stats = ctx.enter_context(tc.tile_pool(name="stats", bufs=3))
+        unused = ctx.enter_context(tc.tile_pool(name="unused", bufs=TILES))
+        xt_psum = ctx.enter_context(tc.psum_pool(name="xt_psum", bufs=2 * PAIRS))
+        h_psum = ctx.enter_context(tc.psum_pool(name="h_psum", bufs=TILES))
+
+        ident = const.tile([P, P], F32)
+        make_identity(nc, ident[:])
+        zero_col = const.tile([P, 1], F32)
+        nc.vector.memset(zero_col[:], 0.0)
+        eps_col = const.tile([P, 1], F32)
+        nc.vector.tensor_scalar(
+            out=eps_col[:], in0=zero_col[:], scalar1=1.0, scalar2=EPS, op0=ALU.mult, op1=ALU.add
+        )
+
+        w_words = const.tile([P, 2 * FEATURES], U8, align_bytes=64)
+        w_scales = const.tile([P, FEATURES], U8, align_bytes=64)
+        nc.vector.memset(w_scales[:].bitcast(I32), 0)
+        bias = const.tile([P, FEATURES], BF16)
+        bias_row = const.tile([P, FEATURES], BF16)
+        nc.vector.memset(bias_row[:], 0.0)
+        ones = const.tile([P, P], BF16)
+        nc.vector.memset(ones[:], 1.0)
+
+        x_pairs = []
+        for g in range(N_GROUPS):
+            x_sb = x_pool.tile([P, TILES, K], BF16, name="x%d" % g)
+            nc.sync.dma_start(out=x_sb[:, :, 0:D_IN], in_=x1_groups[g])
+            nc.sync.dma_start(out=x_sb[:, :, D_IN:K], in_=x2_groups[g])
+            x_pairs.append([x_sb[:, 2 * pair : 2 * pair + 2, :] for pair in range(PAIRS)])
+            if g == 0:
+                nc.sync.dma_start(out=w_words[:].bitcast(I32), in_=W1_words[0].bitcast(I32))
+                for quadrant in range(4):
+                    nc.sync.dma_start(
+                        out=w_scales[32 * quadrant : 32 * quadrant + 4, :].bitcast(I32),
+                        in_=W1_scales[0, 4 * quadrant : 4 * quadrant + 4, :].bitcast(I32),
+                    )
+                nc.sync.dma_start(out=bias_row[0:1, :], in_=b1.rearrange("(o f) -> o f", o=1))
+
+        xt_banks = {}
+        grouped_of = {}
+        product_of = {}
+        h_of = {}
+        row_sum_of = {}
+        sum_sq_of = {}
+        rstd_of = {}
+        shift_of = {}
+        negmean_of = {}
+        result_of = {}
+        y_of = {}
+
+        def spread_bias():
+            product = h_psum.tile([P, FEATURES], F32)
+            nc.tensor.matmul(out=product[:], lhsT=ones[:], rhs=bias_row[:], start=True, stop=True)
+            nc.scalar.copy(out=bias[:], in_=product[:])
+
+        def transpose(g):
+            xt_banks[g] = []
+            for pair in range(PAIRS):
+                x_words = x_pairs[g][pair].bitcast(F32)
+                xt = xt_psum.tile([P, 2, 2, P], F32)
+                for j in range(2):
+                    for u in range(2):
+                        nc.tensor.transpose(xt[:, j, u, :], x_words[:, j, u:WORDS:2], ident[:])
+                xt_banks[g].append(xt)
+
+        def evacuate(g, pair):
+            if g not in grouped_of:
+                grouped = quant.tile([P, TILES * K], BF16, align_bytes=64)
+                grouped_of[g] = grouped
+            words = grouped_of[g][:].bitcast(F32).rearrange("p (j r u) -> p j r u", j=TILES, u=2)
+            nc.scalar.copy(
+                out=words[:, 2 * pair : 2 * pair + 2],
+                in_=xt_banks[g][pair][:].rearrange("p j u r -> p j r u"),
+            )
+
+        def quantise_and_multiply(g, calls):
+            codes = quant.tile([P, TILES * P], U32, align_bytes=64)
+            scales = quant.tile([P, TILES * P], U8, align_bytes=64)
+            product_of[g] = []
+            share = TILES // calls
+            for call in range(calls):
+                rows = slice(call * share * P, (call + 1) * share * P)
+                nc.vector.quantize_mx(
+                    out=codes[:, rows].bitcast(FP8X4),
+                    scales=scales[:, rows],
+                    in_=grouped_of[g][:, call * share * K : (call + 1) * share * K],
+                )
+                for j in range(call * share, (call + 1) * share):
+                    rows = slice(j * P, (j + 1) * P)
+                    product = h_psum.tile([P, FEATURES], F32)
+                    nc.tensor.matmul_mx(
+                        out=product[:],
+                        lhsT=codes[:, rows].bitcast(FP8X4),
+                        lhsT_scale=scales[:, rows],
+                        rhs=w_words[:].bitcast(FP4X4),
+                        rhs_scale=w_scales[:],
+                        start=True,
+                        stop=True,
+                    )
+                    product_of[g].append(product)
+
+        def add_bias(g, tiles):
+            if g not in h_of:
+                h = h_pool.tile([P, TILES, FEATURES], F32)
+                row_sum = stats.tile([P, TILES], F32)
+                h_of[g] = h
+                row_sum_of[g] = row_sum
+            for j in tiles:
+                nc.vector.scalar_tensor_tensor(
+                    out=h_of[g][:, j, :],
+                    in0=product_of[g][j][:],
+                    scalar=1.0,
+                    in1=bias[:],
+                    op0=ALU.mult,
+                    op1=ALU.add,
+                    accum_out=row_sum_of[g][:, j : j + 1],
+                )
+
+        def variance(g):
+            sum_sq = stats.tile([P, TILES], F32)
+            for j in range(TILES):
+                squares = unused.tile([P, FEATURES], F32)
+                nc.scalar.activation(
+                    out=squares[:],
+                    in_=h_of[g][:, j, :],
+                    func=ACT.Square,
+                    bias=row_sum_of[g][:, j : j + 1],
+                    scale=-float(FEATURES),
+                    accum_out=sum_sq[:, j : j + 1],
+                )
+            sum_sq_of[g] = sum_sq
+
+        def inverse_deviation(g):
+            rstd = stats.tile([P, TILES], F32)
+            nc.scalar.activation(
+                out=rstd[:],
+                in_=sum_sq_of[g][:],
+                func=ACT.Abs_reciprocal_sqrt,
+                bias=eps_col[:],
+                scale=1.0 / FEATURES**3,
+            )
+            rstd_of[g] = rstd
+
+        def minus_mean(g):
+            negmean = stats.tile([P, TILES], F32)
+            nc.scalar.activation(
+                out=negmean[:], in_=row_sum_of[g][:], func=ACT.Copy, scale=-1.0 / FEATURES
+            )
+            negmean_of[g] = negmean
+
+        def shift(g, tiles):
+            shifts = stats.tile([P, TILES], F32)
+            for j in tiles:
+                nc.scalar.activation(
+                    out=shifts[:, j : j + 1],
+                    in_=rstd_of[g][:, j : j + 1],
+                    func=ACT.Copy,
+                    scale=negmean_of[g][:, j : j + 1],
+                )
+            shift_of[g] = shifts
+
+        def normalise_on_gpsimd(g, tiles):
+            for j in tiles:
+                nc.gpsimd.tensor_scalar(
+                    out=y_of[g][:, j, :],
+                    in0=h_of[g][:, j, :],
+                    scalar1=negmean_of[g][:, j : j + 1],
+                    scalar2=rstd_of[g][:, j : j + 1],
+                    op0=ALU.add,
+                    op1=ALU.mult,
+                )
+
+        def normalise(g, tiles):
+            if g not in y_of:
+                y = y_pool.tile([P, TILES, FEATURES], F32)
+                y_of[g] = y
+            for j in tiles:
+                nc.scalar.activation(
+                    out=y_of[g][:, j, :],
+                    in_=h_of[g][:, j, :],
+                    func=ACT.Identity,
+                    bias=shift_of[g][:, j : j + 1],
+                    scale=rstd_of[g][:, j : j + 1],
+                )
+
+        def leaky_relu_and_store(g, first, count):
+            if g not in result_of:
+                result = out_pool.tile([P, TILES, FEATURES], F32)
+                result_of[g] = result
+            tiles = slice(first, first + count)
+            flat = y_of[g][:, tiles, :].rearrange("p j f -> p (j f)")
+            nc.vector.scalar_tensor_tensor(
+                out=result_of[g][:, tiles, :].rearrange("p j f -> p (j f)"),
+                in0=flat,
+                scalar=SLOPE,
+                in1=flat,
+                op0=ALU.mult,
+                op1=ALU.max,
+            )
+            nc.sync.dma_start(out=out_groups[g][:, tiles, :], in_=result_of[g][:, tiles, :])
+
+        def run(stage, g, *tiles):
+            if 0 <= g < N_GROUPS:
+                stage(g, *tiles)
+
+        with tc.manual_schedule():
+            transpose(0)
+            evacuate(0, 0)
+            evacuate(0, 1)
+            spread_bias()
+            quantise_and_multiply(0, PAIRS)
+            transpose(1)
+            evacuate(1, 0)
+            evacuate(1, 1)
+            for step in range(0, N_GROUPS + 1):
+                run(transpose, step + 2)
+                if step - 1 == N_GROUPS - 1:
+                    run(normalise, step - 1, (0, 1, 2, 3))
+                else:
+                    run(normalise, step - 1, (0, 1))
+                    run(normalise_on_gpsimd, step - 1, (2, 3))
+                run(add_bias, step, (0, 1, 2, 3))
+                run(quantise_and_multiply, step + 1, 1)
+                run(variance, step)
+                run(minus_mean, step)
+                run(evacuate, step + 2, 0)
+                run(inverse_deviation, step)
+                run(shift, step, (0, 1, 2, 3) if step == N_GROUPS - 1 else (0, 1))
+                run(evacuate, step + 2, 1)
+                if step - 1 == N_GROUPS - 1:
+                    for j in range(TILES):
+                        run(leaky_relu_and_store, step - 1, j, 1)
+                else:
+                    run(leaky_relu_and_store, step - 1, 0, TILES)

@@ -108,14 +108,15 @@ def tile_fcd_pa_t_kernel(tc, input1, input2, W1_words, W1_scales, b1, out):
                         nc.tensor.transpose(xt[:, j, u, :], x_words[:, j, u:WORDS:2], ident[:])
                 xt_banks[g].append(xt)
 
-        def evacuate(g, pair):
+        def evacuate(g, first, count):
             if g not in grouped_of:
                 grouped = quant.tile([P, TILES * K], BF16, align_bytes=64)
                 grouped_of[g] = grouped
             words = grouped_of[g][:].bitcast(F32).rearrange("p (j r u) -> p j r u", j=TILES, u=2)
+            pair, j = divmod(first, 2)
             nc.scalar.copy(
-                out=words[:, 2 * pair : 2 * pair + 2],
-                in_=xt_banks[g][pair][:].rearrange("p j u r -> p j r u"),
+                out=words[:, first : first + count],
+                in_=xt_banks[g][pair][:, j : j + count].rearrange("p j u r -> p j r u"),
             )
 
         def quantise_and_multiply(g, calls):
@@ -250,13 +251,13 @@ def tile_fcd_pa_t_kernel(tc, input1, input2, W1_words, W1_scales, b1, out):
 
         with tc.manual_schedule():
             transpose(0)
-            evacuate(0, 0)
-            evacuate(0, 1)
+            evacuate(0, 0, 2)
+            evacuate(0, 2, 2)
             spread_bias()
             quantise_and_multiply(0, PAIRS)
             transpose(1)
-            evacuate(1, 0)
-            evacuate(1, 1)
+            evacuate(1, 0, 2)
+            evacuate(1, 2, 2)
             for step in range(0, N_GROUPS + 1):
                 run(transpose, step + 2)
                 if step - 1 == N_GROUPS - 1:
@@ -268,10 +269,11 @@ def tile_fcd_pa_t_kernel(tc, input1, input2, W1_words, W1_scales, b1, out):
                 run(quantise_and_multiply, step + 1, 1)
                 run(variance, step)
                 run(minus_mean, step)
-                run(evacuate, step + 2, 0)
+                run(evacuate, step + 2, 0, 2)
                 run(inverse_deviation, step)
+                run(evacuate, step + 2, 2, 1)
                 run(shift, step, (0, 1, 2, 3) if step == N_GROUPS - 1 else (0, 1))
-                run(evacuate, step + 2, 1)
+                run(evacuate, step + 2, 3, 1)
                 if step - 1 == N_GROUPS - 1:
                     for j in range(TILES):
                         run(leaky_relu_and_store, step - 1, j, 1)

@@ -22,9 +22,10 @@ FEATURES = 512
 EPS = 1e-5
 SLOPE = 0.2
 
-TILES = 4
-PAIRS = TILES // 2
-N_GROUPS = ROWS // (TILES * P)
+SIZES = [4] + 7 * [8] + [4]
+N_GROUPS = len(SIZES)
+FIRST_TILE = [sum(SIZES[:g]) for g in range(N_GROUPS)]
+BANKS = 4
 
 FLOPS = 2 * ROWS * K * FEATURES
 
@@ -32,21 +33,21 @@ FLOPS = 2 * ROWS * K * FEATURES
 def tile_fcd_pa_t_kernel(tc, input1, input2, W1_words, W1_scales, b1, out):
     nc = tc.nc
 
-    x1_groups = input1.rearrange("(g p j) o d -> g p j (o d)", p=P, j=TILES)
-    x2_groups = input2.rearrange("(g p j) o d -> g p j (o d)", p=P, j=TILES)
-    out_groups = out.rearrange("(g p j) o f -> g p j (o f)", p=P, j=TILES)
+    def rows_of(array, g):
+        rows = slice(FIRST_TILE[g] * P, (FIRST_TILE[g] + SIZES[g]) * P)
+        return array[rows, :, :].rearrange("(p j) o d -> p j (o d)", j=SIZES[g])
 
     with ExitStack() as ctx:
         const = ctx.enter_context(tc.tile_pool(name="const", bufs=1))
         x_pool = ctx.enter_context(tc.tile_pool(name="x", bufs=1))
         quant = ctx.enter_context(tc.tile_pool(name="quant", bufs=2))
-        h_pool = ctx.enter_context(tc.tile_pool(name="h", bufs=3))
-        y_pool = ctx.enter_context(tc.tile_pool(name="y", bufs=3))
-        out_pool = ctx.enter_context(tc.tile_pool(name="out", bufs=4))
+        h_pool = ctx.enter_context(tc.tile_pool(name="h", bufs=2))
+        y_pool = ctx.enter_context(tc.tile_pool(name="y", bufs=2))
+        out_pool = ctx.enter_context(tc.tile_pool(name="out", bufs=3))
         stats = ctx.enter_context(tc.tile_pool(name="stats", bufs=3))
-        unused = ctx.enter_context(tc.tile_pool(name="unused", bufs=TILES))
-        xt_psum = ctx.enter_context(tc.psum_pool(name="xt_psum", bufs=2 * PAIRS))
-        h_psum = ctx.enter_context(tc.psum_pool(name="h_psum", bufs=TILES))
+        unused = ctx.enter_context(tc.tile_pool(name="unused", bufs=4))
+        xt_psum = ctx.enter_context(tc.psum_pool(name="xt_psum", bufs=BANKS))
+        h_psum = ctx.enter_context(tc.psum_pool(name="h_psum", bufs=BANKS))
 
         ident = const.tile([P, P], F32)
         make_identity(nc, ident[:])
@@ -66,12 +67,12 @@ def tile_fcd_pa_t_kernel(tc, input1, input2, W1_words, W1_scales, b1, out):
         ones = const.tile([P, P], BF16)
         nc.vector.memset(ones[:], 1.0)
 
-        x_pairs = []
+        x_of = []
         for g in range(N_GROUPS):
-            x_sb = x_pool.tile([P, TILES, K], BF16, name="x%d" % g)
-            nc.sync.dma_start(out=x_sb[:, :, 0:D_IN], in_=x1_groups[g])
-            nc.sync.dma_start(out=x_sb[:, :, D_IN:K], in_=x2_groups[g])
-            x_pairs.append([x_sb[:, 2 * pair : 2 * pair + 2, :] for pair in range(PAIRS)])
+            x_sb = x_pool.tile([P, SIZES[g], K], BF16, name="x%d" % g)
+            nc.sync.dma_start(out=x_sb[:, :, 0:D_IN], in_=rows_of(input1, g))
+            nc.sync.dma_start(out=x_sb[:, :, D_IN:K], in_=rows_of(input2, g))
+            x_of.append(x_sb)
             if g == 0:
                 nc.sync.dma_start(out=w_words[:].bitcast(I32), in_=W1_words[0].bitcast(I32))
                 for quadrant in range(4):
@@ -83,6 +84,8 @@ def tile_fcd_pa_t_kernel(tc, input1, input2, W1_words, W1_scales, b1, out):
 
         xt_banks = {}
         grouped_of = {}
+        codes_of = {}
+        scales_of = {}
         product_of = {}
         h_of = {}
         row_sum_of = {}
@@ -100,8 +103,8 @@ def tile_fcd_pa_t_kernel(tc, input1, input2, W1_words, W1_scales, b1, out):
 
         def transpose(g):
             xt_banks[g] = []
-            for pair in range(PAIRS):
-                x_words = x_pairs[g][pair].bitcast(F32)
+            for pair in range(SIZES[g] // 2):
+                x_words = x_of[g][:, 2 * pair : 2 * pair + 2, :].bitcast(F32)
                 xt = xt_psum.tile([P, 2, 2, P], F32)
                 for j in range(2):
                     for u in range(2):
@@ -110,20 +113,36 @@ def tile_fcd_pa_t_kernel(tc, input1, input2, W1_words, W1_scales, b1, out):
 
         def evacuate(g, first, count):
             if g not in grouped_of:
-                grouped = quant.tile([P, TILES * K], BF16, align_bytes=64)
+                grouped = quant.tile([P, SIZES[g] * K], BF16, align_bytes=64)
                 grouped_of[g] = grouped
-            words = grouped_of[g][:].bitcast(F32).rearrange("p (j r u) -> p j r u", j=TILES, u=2)
+            words = grouped_of[g][:].bitcast(F32).rearrange("p (j r u) -> p j r u", j=SIZES[g], u=2)
             pair, j = divmod(first, 2)
             nc.scalar.copy(
                 out=words[:, first : first + count],
                 in_=xt_banks[g][pair][:, j : j + count].rearrange("p j u r -> p j r u"),
             )
 
+        def multiply(g, j):
+            rows = slice(j * P, (j + 1) * P)
+            product = h_psum.tile([P, FEATURES], F32)
+            nc.tensor.matmul_mx(
+                out=product[:],
+                lhsT=codes_of[g][:, rows].bitcast(FP8X4),
+                lhsT_scale=scales_of[g][:, rows],
+                rhs=w_words[:].bitcast(FP4X4),
+                rhs_scale=w_scales[:],
+                start=True,
+                stop=True,
+            )
+            product_of[g].append(product)
+
         def quantise_and_multiply(g, calls):
-            codes = quant.tile([P, TILES * P], U32, align_bytes=64)
-            scales = quant.tile([P, TILES * P], U8, align_bytes=64)
+            codes = quant.tile([P, SIZES[g] * P], U32, align_bytes=64)
+            scales = quant.tile([P, SIZES[g] * P], U8, align_bytes=64)
+            codes_of[g] = codes
+            scales_of[g] = scales
             product_of[g] = []
-            share = TILES // calls
+            share = SIZES[g] // calls
             for call in range(calls):
                 rows = slice(call * share * P, (call + 1) * share * P)
                 nc.vector.quantize_mx(
@@ -131,40 +150,30 @@ def tile_fcd_pa_t_kernel(tc, input1, input2, W1_words, W1_scales, b1, out):
                     scales=scales[:, rows],
                     in_=grouped_of[g][:, call * share * K : (call + 1) * share * K],
                 )
-                for j in range(call * share, (call + 1) * share):
-                    rows = slice(j * P, (j + 1) * P)
-                    product = h_psum.tile([P, FEATURES], F32)
-                    nc.tensor.matmul_mx(
-                        out=product[:],
-                        lhsT=codes[:, rows].bitcast(FP8X4),
-                        lhsT_scale=scales[:, rows],
-                        rhs=w_words[:].bitcast(FP4X4),
-                        rhs_scale=w_scales[:],
-                        start=True,
-                        stop=True,
-                    )
-                    product_of[g].append(product)
+                for j in range(call * share, min((call + 1) * share, BANKS)):
+                    multiply(g, j)
 
-        def add_bias(g, tiles):
-            if g not in h_of:
-                h = h_pool.tile([P, TILES, FEATURES], F32)
-                row_sum = stats.tile([P, TILES], F32)
-                h_of[g] = h
-                row_sum_of[g] = row_sum
-            for j in tiles:
+        def add_bias(g):
+            h = h_pool.tile([P, SIZES[g], FEATURES], F32)
+            row_sum = stats.tile([P, SIZES[g]], F32)
+            h_of[g] = h
+            row_sum_of[g] = row_sum
+            for j in range(SIZES[g]):
                 nc.vector.scalar_tensor_tensor(
-                    out=h_of[g][:, j, :],
+                    out=h[:, j, :],
                     in0=product_of[g][j][:],
                     scalar=1.0,
                     in1=bias[:],
                     op0=ALU.mult,
                     op1=ALU.add,
-                    accum_out=row_sum_of[g][:, j : j + 1],
+                    accum_out=row_sum[:, j : j + 1],
                 )
+                if j + BANKS < SIZES[g]:
+                    multiply(g, j + BANKS)
 
         def variance(g):
-            sum_sq = stats.tile([P, TILES], F32)
-            for j in range(TILES):
+            sum_sq = stats.tile([P, SIZES[g]], F32)
+            for j in range(SIZES[g]):
                 squares = unused.tile([P, FEATURES], F32)
                 nc.scalar.activation(
                     out=squares[:],
@@ -177,7 +186,7 @@ def tile_fcd_pa_t_kernel(tc, input1, input2, W1_words, W1_scales, b1, out):
             sum_sq_of[g] = sum_sq
 
         def inverse_deviation(g):
-            rstd = stats.tile([P, TILES], F32)
+            rstd = stats.tile([P, SIZES[g]], F32)
             nc.scalar.activation(
                 out=rstd[:],
                 in_=sum_sq_of[g][:],
@@ -188,14 +197,14 @@ def tile_fcd_pa_t_kernel(tc, input1, input2, W1_words, W1_scales, b1, out):
             rstd_of[g] = rstd
 
         def minus_mean(g):
-            negmean = stats.tile([P, TILES], F32)
+            negmean = stats.tile([P, SIZES[g]], F32)
             nc.scalar.activation(
                 out=negmean[:], in_=row_sum_of[g][:], func=ACT.Copy, scale=-1.0 / FEATURES
             )
             negmean_of[g] = negmean
 
         def shift(g, tiles):
-            shifts = stats.tile([P, TILES], F32)
+            shifts = stats.tile([P, SIZES[g]], F32)
             for j in tiles:
                 nc.scalar.activation(
                     out=shifts[:, j : j + 1],
@@ -218,7 +227,7 @@ def tile_fcd_pa_t_kernel(tc, input1, input2, W1_words, W1_scales, b1, out):
 
         def normalise(g, tiles):
             if g not in y_of:
-                y = y_pool.tile([P, TILES, FEATURES], F32)
+                y = y_pool.tile([P, SIZES[g], FEATURES], F32)
                 y_of[g] = y
             for j in tiles:
                 nc.scalar.activation(
@@ -231,7 +240,7 @@ def tile_fcd_pa_t_kernel(tc, input1, input2, W1_words, W1_scales, b1, out):
 
         def leaky_relu_and_store(g, first, count):
             if g not in result_of:
-                result = out_pool.tile([P, TILES, FEATURES], F32)
+                result = out_pool.tile([P, SIZES[g], FEATURES], F32)
                 result_of[g] = result
             tiles = slice(first, first + count)
             flat = y_of[g][:, tiles, :].rearrange("p j f -> p (j f)")
@@ -243,7 +252,7 @@ def tile_fcd_pa_t_kernel(tc, input1, input2, W1_words, W1_scales, b1, out):
                 op0=ALU.mult,
                 op1=ALU.max,
             )
-            nc.sync.dma_start(out=out_groups[g][:, tiles, :], in_=result_of[g][:, tiles, :])
+            nc.sync.dma_start(out=rows_of(out, g)[:, tiles, :], in_=result_of[g][:, tiles, :])
 
         def run(stage, g, *tiles):
             if 0 <= g < N_GROUPS:
@@ -254,28 +263,38 @@ def tile_fcd_pa_t_kernel(tc, input1, input2, W1_words, W1_scales, b1, out):
             evacuate(0, 0, 2)
             evacuate(0, 2, 2)
             spread_bias()
-            quantise_and_multiply(0, PAIRS)
+            quantise_and_multiply(0, 2)
             transpose(1)
-            evacuate(1, 0, 2)
-            evacuate(1, 2, 2)
+            for first in range(0, SIZES[1], 2):
+                evacuate(1, first, 2)
             for step in range(0, N_GROUPS + 1):
+                last = N_GROUPS - 1
+                if 0 <= step - 1:
+                    half = SIZES[step - 1] // 2
+                    if step - 1 == last:
+                        normalise(last, range(SIZES[last]))
+                    else:
+                        normalise(step - 1, range(half))
+                        normalise_on_gpsimd(step - 1, range(half, SIZES[step - 1]))
+                run(add_bias, step)
                 run(transpose, step + 2)
-                if step - 1 == N_GROUPS - 1:
-                    run(normalise, step - 1, (0, 1, 2, 3))
-                else:
-                    run(normalise, step - 1, (0, 1))
-                    run(normalise_on_gpsimd, step - 1, (2, 3))
-                run(add_bias, step, (0, 1, 2, 3))
                 run(quantise_and_multiply, step + 1, 1)
                 run(variance, step)
                 run(minus_mean, step)
                 run(evacuate, step + 2, 0, 2)
                 run(inverse_deviation, step)
-                run(evacuate, step + 2, 2, 1)
-                run(shift, step, (0, 1, 2, 3) if step == N_GROUPS - 1 else (0, 1))
-                run(evacuate, step + 2, 3, 1)
-                if step - 1 == N_GROUPS - 1:
-                    for j in range(TILES):
-                        run(leaky_relu_and_store, step - 1, j, 1)
-                else:
-                    run(leaky_relu_and_store, step - 1, 0, TILES)
+                run(evacuate, step + 2, 2, 2)
+                if step <= last:
+                    shift(step, range(SIZES[step] if step == last else SIZES[step] // 2))
+                if step + 2 <= last:
+                    for first in range(4, SIZES[step + 2], 2):
+                        evacuate(step + 2, first, 2)
+                if step - 1 == last:
+                    for j in range(SIZES[last]):
+                        leaky_relu_and_store(last, j, 1)
+                elif step - 1 == last - 1:
+                    half = SIZES[step - 1] // 2
+                    leaky_relu_and_store(step - 1, 0, half)
+                    leaky_relu_and_store(step - 1, half, half)
+                elif step >= 1:
+                    leaky_relu_and_store(step - 1, 0, SIZES[step - 1])

@@ -24,6 +24,12 @@ SLOPE = 0.2
 
 SIZES = [4] + 7 * [8] + [4]
 N_GROUPS = len(SIZES)
+SUMS = range(1, N_GROUPS - 2)
+NORMS = (
+    [((0, 1), (2, 3))]
+    + [((0, 1, 2, 7), (3, 4, 5, 6)) for g in SUMS]
+    + [((0, 1, 2, 3, 4), (5, 6, 7)), ((0, 1, 2, 3), ())]
+)
 FIRST_TILE = [sum(SIZES[:g]) for g in range(N_GROUPS)]
 BANKS = 4
 
@@ -44,6 +50,7 @@ def tile_fcd_pa_t_kernel(tc, input1, input2, W1_words, W1_scales, b1, out):
         h_pool = ctx.enter_context(tc.tile_pool(name="h", bufs=2))
         y_pool = ctx.enter_context(tc.tile_pool(name="y", bufs=2))
         out_pool = ctx.enter_context(tc.tile_pool(name="out", bufs=3))
+        part_pool = ctx.enter_context(tc.tile_pool(name="part", bufs=2))
         stats = ctx.enter_context(tc.tile_pool(name="stats", bufs=3))
         unused = ctx.enter_context(tc.tile_pool(name="unused", bufs=4))
         xt_psum = ctx.enter_context(tc.psum_pool(name="xt_psum", bufs=BANKS))
@@ -94,6 +101,7 @@ def tile_fcd_pa_t_kernel(tc, input1, input2, W1_words, W1_scales, b1, out):
         shift_of = {}
         negmean_of = {}
         result_of = {}
+        part_of = {}
         y_of = {}
 
         def spread_bias():
@@ -238,7 +246,21 @@ def tile_fcd_pa_t_kernel(tc, input1, input2, W1_words, W1_scales, b1, out):
                     scale=rstd_of[g][:, j : j + 1],
                 )
 
-        def leaky_relu_and_store(g, first, count):
+        def negative_part(g, j):
+            part = part_pool.tile([P, FEATURES], F32)
+            nc.scalar.activation(
+                out=part[:], in_=y_of[g][:, j, :], func=ACT.Relu, scale=-(1.0 - SLOPE)
+            )
+            part_of[g] = part
+
+        def add_on_gpsimd(g, j):
+            result = out_pool.tile([P, SIZES[g], FEATURES], F32)
+            result_of[g] = result
+            nc.gpsimd.tensor_tensor(
+                out=result[:, j, :], in0=y_of[g][:, j, :], in1=part_of[g][:], op=ALU.add
+            )
+
+        def leaky_relu(g, first, count):
             if g not in result_of:
                 result = out_pool.tile([P, SIZES[g], FEATURES], F32)
                 result_of[g] = result
@@ -252,6 +274,9 @@ def tile_fcd_pa_t_kernel(tc, input1, input2, W1_words, W1_scales, b1, out):
                 op0=ALU.mult,
                 op1=ALU.max,
             )
+
+        def store(g, first, count):
+            tiles = slice(first, first + count)
             nc.sync.dma_start(out=rows_of(out, g)[:, tiles, :], in_=result_of[g][:, tiles, :])
 
         def run(stage, g, *tiles):
@@ -269,13 +294,17 @@ def tile_fcd_pa_t_kernel(tc, input1, input2, W1_words, W1_scales, b1, out):
                 evacuate(1, first, 2)
             for step in range(0, N_GROUPS + 1):
                 last = N_GROUPS - 1
-                if 0 <= step - 1:
-                    half = SIZES[step - 1] // 2
-                    if step - 1 == last:
-                        normalise(last, range(SIZES[last]))
+                if step >= 1:
+                    by_scalar, by_gpsimd = NORMS[step - 1]
+                    if step - 1 in SUMS:
+                        normalise(step - 1, (7, 0))
+                        negative_part(step - 1, 7)
+                        normalise(step - 1, by_scalar[1:-1])
+                        normalise_on_gpsimd(step - 1, by_gpsimd)
+                        add_on_gpsimd(step - 1, 7)
                     else:
-                        normalise(step - 1, range(half))
-                        normalise_on_gpsimd(step - 1, range(half, SIZES[step - 1]))
+                        normalise(step - 1, by_scalar)
+                        normalise_on_gpsimd(step - 1, by_gpsimd)
                 run(add_bias, step)
                 run(transpose, step + 2)
                 run(quantise_and_multiply, step + 1, 1)
@@ -285,16 +314,19 @@ def tile_fcd_pa_t_kernel(tc, input1, input2, W1_words, W1_scales, b1, out):
                 run(inverse_deviation, step)
                 run(evacuate, step + 2, 2, 2)
                 if step <= last:
-                    shift(step, range(SIZES[step] if step == last else SIZES[step] // 2))
+                    shift(step, NORMS[step][0])
                 if step + 2 <= last:
                     for first in range(4, SIZES[step + 2], 2):
                         evacuate(step + 2, first, 2)
                 if step - 1 == last:
                     for j in range(SIZES[last]):
-                        leaky_relu_and_store(last, j, 1)
+                        leaky_relu(last, j, 1)
+                        store(last, j, 1)
                 elif step - 1 == last - 1:
                     half = SIZES[step - 1] // 2
-                    leaky_relu_and_store(step - 1, 0, half)
-                    leaky_relu_and_store(step - 1, half, half)
+                    for first in (0, half):
+                        leaky_relu(step - 1, first, half)
+                        store(step - 1, first, half)
                 elif step >= 1:
-                    leaky_relu_and_store(step - 1, 0, SIZES[step - 1])
+                    leaky_relu(step - 1, 0, SIZES[step - 1] - (1 if step - 1 in SUMS else 0))
+                    store(step - 1, 0, SIZES[step - 1])

@@ -33,6 +33,8 @@ NORMS = (
 FIRST_TILE = [sum(SIZES[:g]) for g in range(N_GROUPS)]
 BANKS = 4
 
+WARM_UP = 6
+
 FLOPS = 2 * ROWS * K * FEATURES
 
 
@@ -58,6 +60,8 @@ def tile_fcd_pa_t_kernel(tc, input1, input2, W1_words, W1_scales, b1, out):
 
         ident = const.tile([P, P], F32)
         make_identity(nc, ident[:])
+        ones = const.tile([P, FEATURES], BF16)
+        nc.vector.memset(ones[:], 1.0)
         zero_col = const.tile([P, 1], F32)
         nc.vector.memset(zero_col[:], 0.0)
         eps_col = const.tile([P, 1], F32)
@@ -71,8 +75,6 @@ def tile_fcd_pa_t_kernel(tc, input1, input2, W1_words, W1_scales, b1, out):
         bias = const.tile([P, FEATURES], BF16)
         bias_row = const.tile([P, FEATURES], BF16)
         nc.vector.memset(bias_row[:], 0.0)
-        ones = const.tile([P, P], BF16)
-        nc.vector.memset(ones[:], 1.0)
 
         x_of = []
         for g in range(N_GROUPS):
@@ -87,7 +89,7 @@ def tile_fcd_pa_t_kernel(tc, input1, input2, W1_words, W1_scales, b1, out):
                         out=w_scales[32 * quadrant : 32 * quadrant + 4, :].bitcast(I32),
                         in_=W1_scales[0, 4 * quadrant : 4 * quadrant + 4, :].bitcast(I32),
                     )
-                nc.sync.dma_start(out=bias_row[0:1, :], in_=b1.rearrange("(o f) -> o f", o=1))
+                nc.gpsimd.dma_start(out=bias_row[0:1, :], in_=b1.rearrange("(o f) -> o f", o=1))
 
         xt_banks = {}
         grouped_of = {}
@@ -104,10 +106,19 @@ def tile_fcd_pa_t_kernel(tc, input1, input2, W1_words, W1_scales, b1, out):
         part_of = {}
         y_of = {}
 
+        def warm_up():
+            product = h_psum.tile([P, FEATURES], F32)
+            for repeat in range(WARM_UP):
+                nc.tensor.matmul(
+                    out=product[:], lhsT=ones[:, 0:P], rhs=ones[:], start=True, stop=True
+                )
+
         def spread_bias():
             product = h_psum.tile([P, FEATURES], F32)
-            nc.tensor.matmul(out=product[:], lhsT=ones[:], rhs=bias_row[:], start=True, stop=True)
-            nc.scalar.copy(out=bias[:], in_=product[:])
+            nc.tensor.matmul(
+                out=product[:], lhsT=ones[:, 0:P], rhs=bias_row[:], start=True, stop=True
+            )
+            return product
 
         def transpose(g):
             xt_banks[g] = []
@@ -284,11 +295,13 @@ def tile_fcd_pa_t_kernel(tc, input1, input2, W1_words, W1_scales, b1, out):
                 stage(g, *tiles)
 
         with tc.manual_schedule():
+            warm_up()
             transpose(0)
             evacuate(0, 0, 2)
             evacuate(0, 2, 2)
-            spread_bias()
+            spread = spread_bias()
             quantise_and_multiply(0, 2)
+            nc.vector.tensor_copy(out=bias[:], in_=spread[:])
             transpose(1)
             for first in range(0, SIZES[1], 2):
                 evacuate(1, first, 2)

@@ -24,9 +24,10 @@ SLOPE = 0.2
 
 SIZES = [4] + 7 * [8] + [4]
 N_GROUPS = len(SIZES)
-SUMS = range(1, N_GROUPS - 2)
+SUMS = range(2, N_GROUPS - 2)
+HALVED = 1
 NORMS = (
-    [((0, 1), (2, 3))]
+    [((0, 1), (2, 3)), ((0, 1, 2, 3), (4, 5, 6, 7))]
     + [((0, 1, 2, 7), (3, 4, 5, 6)) for g in SUMS]
     + [((0, 1, 2, 3, 4), (5, 6, 7)), ((0, 1, 2, 3), ())]
 )
@@ -58,6 +59,10 @@ def tile_fcd_pa_t_kernel(tc, input1, input2, W1_words, W1_scales, b1, out):
         xt_psum = ctx.enter_context(tc.psum_pool(name="xt_psum", bufs=BANKS))
         h_psum = ctx.enter_context(tc.psum_pool(name="h_psum", bufs=BANKS))
 
+        bias = const.tile([P, FEATURES], BF16)
+        bias_row = const.tile([P, FEATURES], BF16)
+        nc.vector.memset(bias_row[:], 0.0)
+        nc.gpsimd.dma_start(out=bias_row[0:1, :], in_=b1.rearrange("(o f) -> o f", o=1))
         ident = const.tile([P, P], F32)
         make_identity(nc, ident[:])
         ones = const.tile([P, FEATURES], BF16)
@@ -72,9 +77,6 @@ def tile_fcd_pa_t_kernel(tc, input1, input2, W1_words, W1_scales, b1, out):
         w_words = const.tile([P, 2 * FEATURES], U8, align_bytes=64)
         w_scales = const.tile([P, FEATURES], U8, align_bytes=64)
         nc.vector.memset(w_scales[:].bitcast(I32), 0)
-        bias = const.tile([P, FEATURES], BF16)
-        bias_row = const.tile([P, FEATURES], BF16)
-        nc.vector.memset(bias_row[:], 0.0)
 
         x_of = []
         for g in range(N_GROUPS):
@@ -89,7 +91,6 @@ def tile_fcd_pa_t_kernel(tc, input1, input2, W1_words, W1_scales, b1, out):
                         out=w_scales[32 * quadrant : 32 * quadrant + 4, :].bitcast(I32),
                         in_=W1_scales[0, 4 * quadrant : 4 * quadrant + 4, :].bitcast(I32),
                     )
-                nc.gpsimd.dma_start(out=bias_row[0:1, :], in_=b1.rearrange("(o f) -> o f", o=1))
 
         xt_banks = {}
         grouped_of = {}
@@ -155,22 +156,24 @@ def tile_fcd_pa_t_kernel(tc, input1, input2, W1_words, W1_scales, b1, out):
             )
             product_of[g].append(product)
 
-        def quantise_and_multiply(g, calls):
-            codes = quant.tile([P, SIZES[g] * P], U32, align_bytes=64)
-            scales = quant.tile([P, SIZES[g] * P], U8, align_bytes=64)
-            codes_of[g] = codes
-            scales_of[g] = scales
-            product_of[g] = []
-            share = SIZES[g] // calls
-            for call in range(calls):
-                rows = slice(call * share * P, (call + 1) * share * P)
-                nc.vector.quantize_mx(
-                    out=codes[:, rows].bitcast(FP8X4),
-                    scales=scales[:, rows],
-                    in_=grouped_of[g][:, call * share * K : (call + 1) * share * K],
-                )
-                for j in range(call * share, min((call + 1) * share, BANKS)):
-                    multiply(g, j)
+        def quantise(g, first, count):
+            if first == 0:
+                codes = quant.tile([P, SIZES[g] * P], U32, align_bytes=64)
+                scales = quant.tile([P, SIZES[g] * P], U8, align_bytes=64)
+                codes_of[g] = codes
+                scales_of[g] = scales
+                product_of[g] = []
+            rows = slice(first * P, (first + count) * P)
+            nc.vector.quantize_mx(
+                out=codes_of[g][:, rows].bitcast(FP8X4),
+                scales=scales_of[g][:, rows],
+                in_=grouped_of[g][:, first * K : (first + count) * K],
+            )
+
+        def quantise_and_multiply(g):
+            quantise(g, 0, BANKS if g == HALVED else SIZES[g])
+            for j in range(BANKS):
+                multiply(g, j)
 
         def add_bias(g):
             h = h_pool.tile([P, SIZES[g], FEATURES], F32)
@@ -187,7 +190,11 @@ def tile_fcd_pa_t_kernel(tc, input1, input2, W1_words, W1_scales, b1, out):
                     op1=ALU.add,
                     accum_out=row_sum[:, j : j + 1],
                 )
-                if j + BANKS < SIZES[g]:
+                if g == HALVED and j == 1:
+                    quantise(g, BANKS, BANKS)
+                    multiply(g, BANKS)
+                    multiply(g, BANKS + 1)
+                elif j + BANKS < SIZES[g] and not (g == HALVED and j == 0):
                     multiply(g, j + BANKS)
 
         def variance(g):
@@ -300,7 +307,10 @@ def tile_fcd_pa_t_kernel(tc, input1, input2, W1_words, W1_scales, b1, out):
             evacuate(0, 0, 2)
             evacuate(0, 2, 2)
             spread = spread_bias()
-            quantise_and_multiply(0, 2)
+            for first in (0, 2):
+                quantise(0, first, 2)
+                multiply(0, first)
+                multiply(0, first + 1)
             nc.vector.tensor_copy(out=bias[:], in_=spread[:])
             transpose(1)
             for first in range(0, SIZES[1], 2):
@@ -319,8 +329,12 @@ def tile_fcd_pa_t_kernel(tc, input1, input2, W1_words, W1_scales, b1, out):
                         normalise(step - 1, by_scalar)
                         normalise_on_gpsimd(step - 1, by_gpsimd)
                 run(add_bias, step)
-                run(transpose, step + 2)
-                run(quantise_and_multiply, step + 1, 1)
+                if step + 1 == HALVED:
+                    quantise_and_multiply(step + 1)
+                    transpose(step + 2)
+                else:
+                    run(transpose, step + 2)
+                    run(quantise_and_multiply, step + 1)
                 run(variance, step)
                 run(minus_mean, step)
                 run(evacuate, step + 2, 0, 2)

@@ -22,15 +22,11 @@ FEATURES = 512
 EPS = 1e-5
 SLOPE = 0.2
 
-SIZES = [4] + 7 * [8] + [4]
+SIZES = [4]+7*[8]+[4]
 N_GROUPS = len(SIZES)
-SUMS = range(2, N_GROUPS - 2)
+SUMS = range(1,7)
 HALVED = 1
-NORMS = (
-    [((0, 1), (2, 3)), ((0, 1, 2, 3), (4, 5, 6, 7))]
-    + [((0, 1, 2, 7), (3, 4, 5, 6)) for g in SUMS]
-    + [((0, 1, 2, 3, 4), (5, 6, 7)), ((0, 1, 2, 3), ())]
-)
+NORMS = [((),(0,1,2,3))]+6*[((0,1,2,7),(3,4,5,6))]+[((0,1,2,3,4),(5,6,7)),((0,1,2,3),())]
 FIRST_TILE = [sum(SIZES[:g]) for g in range(N_GROUPS)]
 BANKS = 4
 
@@ -171,7 +167,8 @@ def tile_fcd_pa_t_kernel(tc, input1, input2, W1_words, W1_scales, b1, out):
             )
 
         def quantise_and_multiply(g):
-            quantise(g, 0, BANKS if g == HALVED else SIZES[g])
+            if g != HALVED:
+                quantise(g, 0, SIZES[g])
             for j in range(BANKS):
                 multiply(g, j)
 
@@ -190,6 +187,8 @@ def tile_fcd_pa_t_kernel(tc, input1, input2, W1_words, W1_scales, b1, out):
                     op1=ALU.add,
                     accum_out=row_sum[:, j : j + 1],
                 )
+                if g + 1 == HALVED and j == SIZES[g] - 2:
+                    quantise(g + 1, 0, BANKS)
                 if g == HALVED and j == 1:
                     quantise(g, BANKS, BANKS)
                     multiply(g, BANKS)
@@ -307,11 +306,11 @@ def tile_fcd_pa_t_kernel(tc, input1, input2, W1_words, W1_scales, b1, out):
             evacuate(0, 0, 2)
             evacuate(0, 2, 2)
             spread = spread_bias()
+            nc.scalar.copy(out=bias[:], in_=spread[:])
             for first in (0, 2):
                 quantise(0, first, 2)
                 multiply(0, first)
                 multiply(0, first + 1)
-            nc.vector.tensor_copy(out=bias[:], in_=spread[:])
             transpose(1)
             for first in range(0, SIZES[1], 2):
                 evacuate(1, first, 2)
@@ -346,14 +345,13 @@ def tile_fcd_pa_t_kernel(tc, input1, input2, W1_words, W1_scales, b1, out):
                     for first in range(4, SIZES[step + 2], 2):
                         evacuate(step + 2, first, 2)
                 if step - 1 == last:
-                    for j in range(SIZES[last]):
-                        leaky_relu(last, j, 1)
-                        store(last, j, 1)
+                    for first in range(0, SIZES[last], 2):
+                        leaky_relu(last, first, 2)
+                        store(last, first, 2)
                 elif step - 1 == last - 1:
-                    half = SIZES[step - 1] // 2
-                    for first in (0, half):
-                        leaky_relu(step - 1, first, half)
-                        store(step - 1, first, half)
+                    for first in range(0, SIZES[step - 1], 2):
+                        leaky_relu(step - 1, first, 2)
+                        store(step - 1, first, 2)
                 elif step >= 1:
                     leaky_relu(step - 1, 0, SIZES[step - 1] - (1 if step - 1 in SUMS else 0))
                     store(step - 1, 0, SIZES[step - 1])

from contextlib import ExitStack

import concourse.mybir as mybir
from concourse.masks import make_identity

F32 = mybir.dt.float32
BF16 = mybir.dt.bfloat16
I32 = mybir.dt.int32
U32 = mybir.dt.uint32
U8 = mybir.dt.uint8
FP8X4 = mybir.dt.float8_e4m3fn_x4
FP4X4 = mybir.dt.float4_e2m1fn_x4
ACT = mybir.ActivationFunctionType
ALU = mybir.AluOpType

P = 128
ROWS = 8192
D_IN = 256
K = 2 * D_IN
WORDS = K // 2
FEATURES = 512
EPS = 1e-5
SLOPE = 0.2

SIZES = [4]+7*[8]+[4]
N_GROUPS = len(SIZES)
SUMS = range(1,7)
HALVED = 1
NORMS = [((),(0,1,2,3))]+6*[((0,1,2,7),(3,4,5,6))]+[((0,1,2,3,4),(5,6,7)),((0,1,2,3),())]
FIRST_TILE = [sum(SIZES[:g]) for g in range(N_GROUPS)]
BANKS = 4

WARM_UP = 6

FLOPS = 2 * ROWS * K * FEATURES


def tile_fcd_pa_t_kernel(tc, input1, input2, W1_words, W1_scales, b1, out):
    nc = tc.nc

    def rows_of(array, g):
        rows = slice(FIRST_TILE[g] * P, (FIRST_TILE[g] + SIZES[g]) * P)
        return array[rows, :, :].rearrange("(p j) o d -> p j (o d)", j=SIZES[g])

    with ExitStack() as ctx:
        const = ctx.enter_context(tc.tile_pool(name="const", bufs=1))
        x_pool = ctx.enter_context(tc.tile_pool(name="x", bufs=1))
        quant = ctx.enter_context(tc.tile_pool(name="quant", bufs=2))
        h_pool = ctx.enter_context(tc.tile_pool(name="h", bufs=2))
        y_pool = ctx.enter_context(tc.tile_pool(name="y", bufs=2))
        out_pool = ctx.enter_context(tc.tile_pool(name="out", bufs=3))
        part_pool = ctx.enter_context(tc.tile_pool(name="part", bufs=2))
        stats = ctx.enter_context(tc.tile_pool(name="stats", bufs=3))
        unused = ctx.enter_context(tc.tile_pool(name="unused", bufs=4))
        xt_psum = ctx.enter_context(tc.psum_pool(name="xt_psum", bufs=BANKS))
        h_psum = ctx.enter_context(tc.psum_pool(name="h_psum", bufs=BANKS))

        bias = const.tile([P, FEATURES], BF16)
        bias_row = const.tile([P, FEATURES], BF16)
        nc.vector.memset(bias_row[:], 0.0)
        nc.gpsimd.dma_start(out=bias_row[0:1, :], in_=b1.rearrange("(o f) -> o f", o=1))
        ident = const.tile([P, P], F32)
        make_identity(nc, ident[:])
        ones = const.tile([P, FEATURES], BF16)
        nc.vector.memset(ones[:], 1.0)
        zero_col = const.tile([P, 1], F32)
        nc.vector.memset(zero_col[:], 0.0)
        eps_col = const.tile([P, 1], F32)
        nc.vector.tensor_scalar(
            out=eps_col[:], in0=zero_col[:], scalar1=1.0, scalar2=EPS, op0=ALU.mult, op1=ALU.add
        )

        w_words = const.tile([P, 2 * FEATURES], U8, align_bytes=64)
        w_scales = const.tile([P, FEATURES], U8, align_bytes=64)
        nc.vector.memset(w_scales[:].bitcast(I32), 0)

        x_of = []
        for g in range(N_GROUPS):
            x_sb = x_pool.tile([P, SIZES[g], K], BF16, name="x%d" % g)
            nc.sync.dma_start(out=x_sb[:, :, 0:D_IN], in_=rows_of(input1, g))
            nc.sync.dma_start(out=x_sb[:, :, D_IN:K], in_=rows_of(input2, g))
            x_of.append(x_sb)
            if g == 0:
                nc.sync.dma_start(out=w_words[:].bitcast(I32), in_=W1_words[0].bitcast(I32))
                for quadrant in range(4):
                    nc.sync.dma_start(
                        out=w_scales[32 * quadrant : 32 * quadrant + 4, :].bitcast(I32),
                        in_=W1_scales[0, 4 * quadrant : 4 * quadrant + 4, :].bitcast(I32),
                    )

        xt_banks = {}
        grouped_of = {}
        codes_of = {}
        scales_of = {}
        product_of = {}
        h_of = {}
        row_sum_of = {}
        sum_sq_of = {}
        rstd_of = {}
        shift_of = {}
        negmean_of = {}
        result_of = {}
        part_of = {}
        y_of = {}

        def warm_up():
            product = h_psum.tile([P, FEATURES], F32)
            for repeat in range(WARM_UP):
                nc.tensor.matmul(
                    out=product[:], lhsT=ones[:, 0:P], rhs=ones[:], start=True, stop=True
                )

        def spread_bias():
            product = h_psum.tile([P, FEATURES], F32)
            nc.tensor.matmul(
                out=product[:], lhsT=ones[:, 0:P], rhs=bias_row[:], start=True, stop=True
            )
            return product

        def transpose(g):
            xt_banks[g] = []
            for pair in range(SIZES[g] // 2):
                x_words = x_of[g][:, 2 * pair : 2 * pair + 2, :].bitcast(F32)
                xt = xt_psum.tile([P, 2, 2, P], F32)
                for j in range(2):
                    for u in range(2):
                        nc.tensor.transpose(xt[:, j, u, :], x_words[:, j, u:WORDS:2], ident[:])
                xt_banks[g].append(xt)

        def evacuate(g, first, count):
            if g not in grouped_of:
                grouped = quant.tile([P, SIZES[g] * K], BF16, align_bytes=64)
                grouped_of[g] = grouped
            words = grouped_of[g][:].bitcast(F32).rearrange("p (j r u) -> p j r u", j=SIZES[g], u=2)
            pair, j = divmod(first, 2)
            nc.scalar.copy(
                out=words[:, first : first + count],
                in_=xt_banks[g][pair][:, j : j + count].rearrange("p j u r -> p j r u"),
            )

        def multiply(g, j):
            rows = slice(j * P, (j + 1) * P)
            product = h_psum.tile([P, FEATURES], F32)
            nc.tensor.matmul_mx(
                out=product[:],
                lhsT=codes_of[g][:, rows].bitcast(FP8X4),
                lhsT_scale=scales_of[g][:, rows],
                rhs=w_words[:].bitcast(FP4X4),
                rhs_scale=w_scales[:],
                start=True,
                stop=True,
            )
            product_of[g].append(product)

        def quantise(g, first, count):
            if first == 0:
                codes = quant.tile([P, SIZES[g] * P], U32, align_bytes=64)
                scales = quant.tile([P, SIZES[g] * P], U8, align_bytes=64)
                codes_of[g] = codes
                scales_of[g] = scales
                product_of[g] = []
            rows = slice(first * P, (first + count) * P)
            nc.vector.quantize_mx(
                out=codes_of[g][:, rows].bitcast(FP8X4),
                scales=scales_of[g][:, rows],
                in_=grouped_of[g][:, first * K : (first + count) * K],
            )

        def quantise_and_multiply(g):
            if g != HALVED:
                quantise(g, 0, SIZES[g])
            for j in range(BANKS):
                multiply(g, j)

        def add_bias(g):
            h = h_pool.tile([P, SIZES[g], FEATURES], F32)
            row_sum = stats.tile([P, SIZES[g]], F32)
            h_of[g] = h
            row_sum_of[g] = row_sum
            for j in range(SIZES[g]):
                nc.vector.scalar_tensor_tensor(
                    out=h[:, j, :],
                    in0=product_of[g][j][:],
                    scalar=1.0,
                    in1=bias[:],
                    op0=ALU.mult,
                    op1=ALU.add,
                    accum_out=row_sum[:, j : j + 1],
                )
                if g + 1 == HALVED and j == SIZES[g] - 2:
                    quantise(g + 1, 0, BANKS)
                if g == HALVED and j == 1:
                    quantise(g, BANKS, BANKS)
                    multiply(g, BANKS)
                    multiply(g, BANKS + 1)
                elif j + BANKS < SIZES[g] and not (g == HALVED and j == 0):
                    multiply(g, j + BANKS)

        def variance(g):
            sum_sq = stats.tile([P, SIZES[g]], F32)
            for j in range(SIZES[g]):
                squares = unused.tile([P, FEATURES], F32)
                nc.scalar.activation(
                    out=squares[:],
                    in_=h_of[g][:, j, :],
                    func=ACT.Square,
                    bias=row_sum_of[g][:, j : j + 1],
                    scale=-float(FEATURES),
                    accum_out=sum_sq[:, j : j + 1],
                )
            sum_sq_of[g] = sum_sq

        def inverse_deviation(g):
            rstd = stats.tile([P, SIZES[g]], F32)
            nc.scalar.activation(
                out=rstd[:],
                in_=sum_sq_of[g][:],
                func=ACT.Abs_reciprocal_sqrt,
                bias=eps_col[:],
                scale=1.0 / FEATURES**3,
            )
            rstd_of[g] = rstd

        def minus_mean(g):
            negmean = stats.tile([P, SIZES[g]], F32)
            nc.scalar.activation(
                out=negmean[:], in_=row_sum_of[g][:], func=ACT.Copy, scale=-1.0 / FEATURES
            )
            negmean_of[g] = negmean

        def shift(g, tiles):
            shifts = stats.tile([P, SIZES[g]], F32)
            for j in tiles:
                nc.scalar.activation(
                    out=shifts[:, j : j + 1],
                    in_=rstd_of[g][:, j : j + 1],
                    func=ACT.Copy,
                    scale=negmean_of[g][:, j : j + 1],
                )
            shift_of[g] = shifts

        def normalise_on_gpsimd(g, tiles):
            for j in tiles:
                nc.gpsimd.tensor_scalar(
                    out=y_of[g][:, j, :],
                    in0=h_of[g][:, j, :],
                    scalar1=negmean_of[g][:, j : j + 1],
                    scalar2=rstd_of[g][:, j : j + 1],
                    op0=ALU.add,
                    op1=ALU.mult,
                )

        def normalise(g, tiles):
            if g not in y_of:
                y = y_pool.tile([P, SIZES[g], FEATURES], F32)
                y_of[g] = y
            for j in tiles:
                nc.scalar.activation(
                    out=y_of[g][:, j, :],
                    in_=h_of[g][:, j, :],
                    func=ACT.Identity,
                    bias=shift_of[g][:, j : j + 1],
                    scale=rstd_of[g][:, j : j + 1],
                )

        def negative_part(g, j):
            part = part_pool.tile([P, FEATURES], F32)
            nc.scalar.activation(
                out=part[:], in_=y_of[g][:, j, :], func=ACT.Relu, scale=-(1.0 - SLOPE)
            )
            part_of[g] = part

        def add_on_gpsimd(g, j):
            result = out_pool.tile([P, SIZES[g], FEATURES], F32)
            result_of[g] = result
            nc.gpsimd.tensor_tensor(
                out=result[:, j, :], in0=y_of[g][:, j, :], in1=part_of[g][:], op=ALU.add
            )

        def leaky_relu(g, first, count):
            if g not in result_of:
                result = out_pool.tile([P, SIZES[g], FEATURES], F32)
                result_of[g] = result
            tiles = slice(first, first + count)
            flat = y_of[g][:, tiles, :].rearrange("p j f -> p (j f)")
            nc.vector.scalar_tensor_tensor(
                out=result_of[g][:, tiles, :].rearrange("p j f -> p (j f)"),
                in0=flat,
                scalar=SLOPE,
                in1=flat,
                op0=ALU.mult,
                op1=ALU.max,
            )

        def store(g, first, count):
            tiles = slice(first, first + count)
            nc.sync.dma_start(out=rows_of(out, g)[:, tiles, :], in_=result_of[g][:, tiles, :])

        def run(stage, g, *tiles):
            if 0 <= g < N_GROUPS:
                stage(g, *tiles)

        with tc.manual_schedule():
            warm_up()
            transpose(0)
            evacuate(0, 0, 2)
            evacuate(0, 2, 2)
            spread = spread_bias()
            nc.scalar.copy(out=bias[:], in_=spread[:])
            for first in (0, 2):
                quantise(0, first, 2)
                multiply(0, first)
                multiply(0, first + 1)
            transpose(1)
            for first in range(0, SIZES[1], 2):
                evacuate(1, first, 2)
            for step in range(0, N_GROUPS + 1):
                last = N_GROUPS - 1
                if step >= 1:
                    by_scalar, by_gpsimd = NORMS[step - 1]
                    if step - 1 in SUMS:
                        normalise(step - 1, (7, 0))
                        negative_part(step - 1, 7)
                        normalise(step - 1, by_scalar[1:-1])
                        normalise_on_gpsimd(step - 1, by_gpsimd)
                        add_on_gpsimd(step - 1, 7)
                    else:
                        normalise(step - 1, by_scalar)
                        normalise_on_gpsimd(step - 1, by_gpsimd)
                run(add_bias, step)
                if step + 1 == HALVED:
                    quantise_and_multiply(step + 1)
                    transpose(step + 2)
                else:
                    run(transpose, step + 2)
                    run(quantise_and_multiply, step + 1)
                run(variance, step)
                run(minus_mean, step)
                run(evacuate, step + 2, 0, 2)
                run(inverse_deviation, step)
                run(evacuate, step + 2, 2, 2)
                if step <= last:
                    shift(step, NORMS[step][0])
                if step + 2 <= last:
                    for first in range(4, SIZES[step + 2], 2):
                        evacuate(step + 2, first, 2)
                if step - 1 == last:
                    for first in range(0, SIZES[last], 2):
                        leaky_relu(last, first, 2)
                        store(last, first, 2)
                elif step - 1 == last - 1:
                    for first in range(0, SIZES[step - 1], 2):
                        leaky_relu(step - 1, first, 2)
                        store(step - 1, first, 2)
                elif step >= 1:
                    leaky_relu(step - 1, 0, SIZES[step - 1] - (1 if step - 1 in SUMS else 0))
                    store(step - 1, 0, SIZES[step - 1])
